import numpy as np
import ml_dtypes


def mxq(x, axis, fmt="e4m3"):
    dtype, down = {"e4m3": (ml_dtypes.float8_e4m3fn, 7), "e5m2": (ml_dtypes.float8_e5m2, 14)}[fmt]
    v = np.moveaxis(np.asarray(x, np.float32).astype(ml_dtypes.bfloat16).astype(np.float64), axis, -1)
    blocks = v.reshape(v.shape[:-1] + (-1, 32))
    amax = np.abs(blocks).max(-1, keepdims=True)
    byte = np.maximum(np.where(amax > 0, np.frexp(amax)[1] - 1 + 127, 0) - down, 1)
    scale = np.exp2(byte - 127.0)
    codes = (blocks / scale).astype(np.float32).astype(dtype).astype(np.float64)
    return np.moveaxis((codes * scale).reshape(v.shape), -1, axis)


WIDE = False


def mx_kscale(k):
    if not WIDE:
        return np.ones(k)
    levels = np.array([10, -10, 5, -5, 0])
    a = np.random.permutation(np.resize(levels, k // 512 * 4)).reshape(k // 512, 4)
    idx = np.arange(k)
    return np.exp2(a[idx // 512, idx % 128 // 32])


BF16 = ml_dtypes.bfloat16


def bf(x):
    return np.asarray(x, np.float32).astype(BF16)


def f64(x):
    return np.asarray(x).astype(np.float64)


B, C, H, W = 3, 512, 32, 32
BETA_MIN = 1e-06
REPARAM_OFFSET = 2.0 ** (-18)
PEDESTAL = REPARAM_OFFSET ** 2
BETA_BOUND = (BETA_MIN + PEDESTAL) ** 0.5
GAMMA_BOUND = REPARAM_OFFSET


def setup_inputs():
    t = np.exp2(np.round(np.log2(mx_kscale(C)) / 2))
    amp = np.exp(0.5 * np.random.standard_normal((B, 1, H, W)))
    return {"inputs": bf(np.random.standard_normal((B, C, H, W)) * amp * t[None, :, None, None]),
            "beta": bf((0.5 + np.random.standard_normal(C)) * t),
            "gamma": bf(np.random.standard_normal((C, C)) * 1.4 / np.sqrt(C) * t[:, None] / t[None, :])}


def reference(inputs, beta, gamma):
    x = f64(inputs)
    beta_c = np.maximum(f64(beta), BETA_BOUND) ** 2 - PEDESTAL
    gamma_c = np.maximum(f64(gamma), GAMMA_BOUND) ** 2 - PEDESTAL
    x2 = (x ** 2).reshape(B, C, H * W)
    norm = (mxq(gamma_c, 1, "e4m3") @ mxq(x2, 1, "e4m3")).reshape(B, C, H, W)
    norm = np.sqrt(norm + beta_c[None, :, None, None])
    return x / norm

@@ -1,0 +1,218 @@
+from contextlib import ExitStack
+
+import concourse.mybir as mybir
+from concourse.masks import make_identity
+
+F32 = mybir.dt.float32
+BF16 = mybir.dt.bfloat16
+U32 = mybir.dt.uint32
+U8 = mybir.dt.uint8
+FP8X4 = mybir.dt.float8_e4m3fn_x4
+ALU = mybir.AluOpType
+ACT = mybir.ActivationFunctionType
+
+P = 128
+PACK = 4
+BATCH = 3
+CH = 512
+PIX = 1024
+HALF = 512
+
+FLOPS = 2 * CH * CH * BATCH * PIX
+
+PEDESTAL = 2.0 ** -36
+GAMMA_BOUND = 2.0 ** -18
+BETA_BOUND = (1e-06 + PEDESTAL) ** 0.5
+
+PINNED = True
+S_COLS_FIRST = 512
+S_COLS = 320
+
+
+def tile_gdn_kernel(tc, inputs, beta, gamma, out):
+    nc = tc.nc
+    x_dram = inputs.rearrange("b (p j) h w -> b p j (h w)", j=PACK)
+    o_dram = out.rearrange("b (p j) h w -> b p j (h w)", j=PACK)
+    g_dram = gamma.rearrange("(m j) c -> m (j c)", j=PACK)
+    b_dram = beta.rearrange("(p j) -> p j", j=PACK)
+
+    with ExitStack() as ctx:
+        keep = ctx.enter_context(tc.tile_pool(name="keep", bufs=1))
+        rot = ctx.enter_context(tc.tile_pool(name="rot", bufs=4))
+        psum = ctx.enter_context(tc.psum_pool(name="psum", bufs=8))
+        if PINNED:
+            ctx.enter_context(tc.manual_schedule())
+
+        b_sb = keep.tile([P, PACK], BF16, name="b_sb")
+        nc.scalar.dma_start(out=b_sb[:], in_=b_dram)
+        g_sb = keep.tile([P, PACK * CH], BF16, name="g_sb")
+        nc.sync.dma_start(out=g_sb[:], in_=g_dram)
+        x0 = []
+        for h in range(2):
+            xt = keep.tile([P, PACK, HALF], BF16, name="x0h%d" % h)
+            nc.sync.dma_start(out=xt[:], in_=x_dram[0][:, :, h * HALF:(h + 1) * HALF])
+            x0.append(xt)
+        x_full = {}
+        for b in range(1, BATCH):
+            xt = keep.tile([P, PACK, PIX], BF16, name="x%d" % b)
+            nc.sync.dma_start(out=xt[:], in_=x_dram[b])
+            x_full[b] = xt
+
+        def x_half(b, h):
+            if b == 0:
+                return x0[h][:]
+            return x_full[b][:, :, h * HALF:(h + 1) * HALF]
+
+        ones = keep.tile([P, 1], F32, name="ones")
+        nc.vector.memset(ones[:], 1.0)
+        negb = keep.tile([P, 1], F32, name="negb")
+        nc.vector.memset(negb[:], -GAMMA_BOUND)
+        warm = keep.tile([P, 1], F32, name="warm")
+        nc.scalar.activation(out=warm[:], in_=ones[:], func=ACT.Abs_reciprocal_sqrt)
+        ident = keep.tile([P, P], F32, name="ident")
+        make_identity(nc, ident[:])
+
+        xg = {}
+        xc = {}
+        xs = {}
+        for b in range(BATCH):
+            for h in range(2):
+                xg[(b, h)] = keep.tile([P, HALF, PACK], BF16, name="xg%d%d" % (b, h), align_bytes=64)
+                xc[(b, h)] = keep.tile([P, HALF], U32, name="xc%d%d" % (b, h), align_bytes=64)
+                xs[(b, h)] = keep.tile([P, HALF], U8, name="xs%d%d" % (b, h), align_bytes=64)
+        g_r = keep.tile([P, PACK * CH], F32, name="g_r")
+        g_c = keep.tile([P, PACK * CH], BF16, name="g_c", align_bytes=64)
+        g_codes = keep.tile([P, CH], U32, name="g_codes", align_bytes=64)
+        g_scales = keep.tile([P, CH], U8, name="g_scales", align_bytes=64)
+
+        def square(eng, b, h, n0, n1):
+            if n1 <= n0:
+                return
+            src = x_half(b, h)[:, :, n0:n1].rearrange("p t (c i) -> p c t i", i=4)
+            dst = xg[(b, h)][:, n0:n1, :].rearrange("p (c i) t -> p c t i", i=4)
+            if eng == "S":
+                nc.scalar.activation(out=dst, in_=src, func=ACT.Square)
+            else:
+                nc.vector.tensor_tensor(out=dst, in0=src, in1=src, op=ALU.mult)
+
+        def quantise_x(b, h):
+            nc.vector.quantize_mx(
+                out=xc[(b, h)][:].bitcast(FP8X4),
+                scales=xs[(b, h)][:],
+                in_=xg[(b, h)][:].rearrange("p n t -> p (n t)"),
+            )
+
+        g_words = g_sb[:].bitcast(F32).rearrange("m (j q u) -> m j u q", j=PACK, u=2)
+        g_t = []
+        for j in range(PACK):
+            gt = psum.tile([P, HALF], F32, tag="bank", name="gt%d" % j)
+            for u in range(2):
+                nc.tensor.transpose(gt[:, u * P:(u + 1) * P], g_words[:, j, u, :], ident[:])
+            g_t.append(gt)
+
+        def clamp_gamma(eng, j):
+            src = g_t[j][:, 0:2 * P].bitcast(BF16).rearrange("q (u m e) -> q m u e", u=2, e=2)
+            dst = g_r[:, j * CH:(j + 1) * CH].rearrange("q (m u e) -> q m u e", u=2, e=2)
+            if eng == "S":
+                nc.scalar.activation(out=dst, in_=src, func=ACT.Relu, bias=negb[:, 0:1], scale=1.0)
+            else:
+                nc.vector.tensor_scalar(
+                    out=dst, in0=src, scalar1=GAMMA_BOUND, scalar2=GAMMA_BOUND, op0=ALU.max, op1=ALU.subtract
+                )
+
+        def finish_gamma(a, b):
+            nc.vector.scalar_tensor_tensor(
+                out=g_c[:, a:b], in0=g_r[:, a:b], scalar=2.0 * GAMMA_BOUND, in1=g_r[:, a:b],
+                op0=ALU.add, op1=ALU.mult,
+            )
+
+        def quantise_gamma(a, b):
+            nc.vector.quantize_mx(
+                out=g_codes[:, a // PACK:b // PACK].bitcast(FP8X4),
+                scales=g_scales[:, a // PACK:b // PACK],
+                in_=g_c[:, a:b],
+            )
+
+        clamp_gamma("V", 0)
+        clamp_gamma("V", 1)
+        clamp_gamma("S", 2)
+        clamp_gamma("S", 3)
+        finish_gamma(0, 2 * CH)
+        square("S", 0, 0, 0, S_COLS_FIRST)
+        square("V", 0, 0, S_COLS_FIRST, HALF)
+        finish_gamma(2 * CH, 4 * CH)
+        quantise_gamma(0, 2 * CH)
+        quantise_gamma(2 * CH, 4 * CH)
+        quantise_x(0, 0)
+
+        b_m = keep.tile([P, PACK], F32, name="b_m")
+        nc.vector.tensor_scalar(out=b_m[:], in0=b_sb[:], scalar1=BETA_BOUND, scalar2=None, op0=ALU.max)
+        b_q = keep.tile([P, PACK], F32, name="b_q")
+        nc.vector.tensor_tensor(out=b_q[:], in0=b_m[:], in1=b_m[:], op=ALU.mult)
+        b_c = keep.tile([P, PACK], F32, name="b_c")
+        nc.vector.tensor_scalar(out=b_c[:], in0=b_q[:], scalar1=PEDESTAL, scalar2=None, op0=ALU.subtract)
+
+        square("S", 0, 1, 0, S_COLS)
+        square("V", 0, 1, S_COLS, HALF)
+        quantise_x(0, 1)
+
+        units = [(b, j) for b in range(BATCH) for j in range(PACK)]
+        acc = {}
+
+        def matmuls(u):
+            b, j = units[u]
+            for h in range(2):
+                ps = psum.tile([P, HALF], F32, tag="bank", name="acc%d_%d" % (u, h))
+                nc.tensor.matmul_mx(
+                    out=ps[:],
+                    lhsT=g_codes[:, j * P:(j + 1) * P].bitcast(FP8X4),
+                    lhsT_scale=g_scales[:, j * P:(j + 1) * P],
+                    rhs=xc[(b, h)][:].bitcast(FP8X4),
+                    rhs_scale=xs[(b, h)][:],
+                    start=True,
+                    stop=True,
+                )
+                acc[(u, h)] = ps
+
+        issued = 0
+        for u in range(3):
+            matmuls(u)
+            issued = u + 1
+
+        for u in range(len(units)):
+            b, j = units[u]
+            step = u % PACK
+            limit = min(len(units), u + 4)
+            if step < 3:
+                limit = min(limit, (b + 1) * PACK)
+            while issued < limit:
+                matmuls(issued)
+                issued += 1
+
+            rn = rot.tile([P, PIX], F32, tag="rn", name="rn%d" % u)
+            for h in range(2):
+                nc.scalar.activation(
+                    out=rn[:, h * HALF:(h + 1) * HALF], in_=acc[(u, h)][:],
+                    func=ACT.Abs_reciprocal_sqrt, bias=b_c[:, j:j + 1], scale=1.0,
+                )
+            if b + 1 < BATCH and step < 2:
+                square("S", b + 1, step, 0, S_COLS)
+                square("V", b + 1, step, S_COLS, HALF)
+
+            o_sb = rot.tile([P, PIX], F32, tag="o", name="o%d" % u, bufs=6)
+            last = u == len(units) - 1
+            if b == 0 or last:
+                for h in range(2):
+                    cols = slice(h * HALF, (h + 1) * HALF)
+                    nc.vector.tensor_tensor(
+                        out=o_sb[:, cols], in0=x_half(b, h)[:, j, :], in1=rn[:, cols], op=ALU.mult
+                    )
+                    if last:
+                        nc.sync.dma_start(out=o_dram[b][:, j, cols], in_=o_sb[:, cols])
+            else:
+                nc.vector.tensor_tensor(out=o_sb[:], in0=x_full[b][:, j, :], in1=rn[:], op=ALU.mult)
+            if not last:
+                nc.sync.dma_start(out=o_dram[b][:, j, :], in_=o_sb[:])
+
+            if b + 1 < BATCH and 1 <= step < 3:
+                quantise_x(b + 1, step - 1)

@@ -24,7 +24,7 @@ PEDESTAL = 2.0 ** -36
 GAMMA_BOUND = 2.0 ** -18
 BETA_BOUND = (1e-06 + PEDESTAL) ** 0.5
 
-PINNED = True
+PINNED = False
 S_COLS_FIRST = 512
 S_COLS = 320
 

@@ -24,16 +24,15 @@ PEDESTAL = 2.0 ** -36
 GAMMA_BOUND = 2.0 ** -18
 BETA_BOUND = (1e-06 + PEDESTAL) ** 0.5
 
-PINNED = False
-S_COLS_FIRST = 512
-S_COLS = 320
+PINNED = True
+S_COLS = (384, 384, 320)
 
 
 def tile_gdn_kernel(tc, inputs, beta, gamma, out):
     nc = tc.nc
     x_dram = inputs.rearrange("b (p j) h w -> b p j (h w)", j=PACK)
     o_dram = out.rearrange("b (p j) h w -> b p j (h w)", j=PACK)
-    g_dram = gamma.rearrange("(m j) c -> m (j c)", j=PACK)
+    g_dram = gamma.rearrange("(m j) c -> m j c", j=PACK)
     b_dram = beta.rearrange("(p j) -> p j", j=PACK)
 
     with ExitStack() as ctx:
@@ -45,10 +44,12 @@ def tile_gdn_kernel(tc, inputs, beta, gamma, out):
 
         b_sb = keep.tile([P, PACK], BF16, name="b_sb")
         nc.scalar.dma_start(out=b_sb[:], in_=b_dram)
-        g_sb = keep.tile([P, PACK * CH], BF16, name="g_sb")
-        nc.sync.dma_start(out=g_sb[:], in_=g_dram)
+        g_sb = []
         x0 = []
         for h in range(2):
+            gh = keep.tile([P, 2, CH], BF16, name="g_sb%d" % h)
+            nc.sync.dma_start(out=gh[:], in_=g_dram[:, 2 * h:2 * h + 2, :])
+            g_sb.append(gh)
             xt = keep.tile([P, PACK, HALF], BF16, name="x0h%d" % h)
             nc.sync.dma_start(out=xt[:], in_=x_dram[0][:, :, h * HALF:(h + 1) * HALF])
             x0.append(xt)
@@ -102,12 +103,15 @@ def tile_gdn_kernel(tc, inputs, beta, gamma, out):
                 in_=xg[(b, h)][:].rearrange("p n t -> p (n t)"),
             )
 
-        g_words = g_sb[:].bitcast(F32).rearrange("m (j q u) -> m j u q", j=PACK, u=2)
         g_t = []
         for j in range(PACK):
+            g_words = (
+                g_sb[j // 2][:].rearrange("m j c -> m (j c)").bitcast(F32)
+                .rearrange("m (j q u) -> m j u q", j=2, u=2)
+            )
             gt = psum.tile([P, HALF], F32, tag="bank", name="gt%d" % j)
             for u in range(2):
-                nc.tensor.transpose(gt[:, u * P:(u + 1) * P], g_words[:, j, u, :], ident[:])
+                nc.tensor.transpose(gt[:, u * P:(u + 1) * P], g_words[:, j % 2, u, :], ident[:])
             g_t.append(gt)
 
         def clamp_gamma(eng, j):
@@ -133,31 +137,19 @@ def tile_gdn_kernel(tc, inputs, beta, gamma, out):
                 in_=g_c[:, a:b],
             )
 
-        clamp_gamma("V", 0)
-        clamp_gamma("V", 1)
-        clamp_gamma("S", 2)
-        clamp_gamma("S", 3)
-        finish_gamma(0, 2 * CH)
-        square("S", 0, 0, 0, S_COLS_FIRST)
-        square("V", 0, 0, S_COLS_FIRST, HALF)
-        finish_gamma(2 * CH, 4 * CH)
-        quantise_gamma(0, 2 * CH)
-        quantise_gamma(2 * CH, 4 * CH)
-        quantise_x(0, 0)
-
-        b_m = keep.tile([P, PACK], F32, name="b_m")
-        nc.vector.tensor_scalar(out=b_m[:], in0=b_sb[:], scalar1=BETA_BOUND, scalar2=None, op0=ALU.max)
-        b_q = keep.tile([P, PACK], F32, name="b_q")
-        nc.vector.tensor_tensor(out=b_q[:], in0=b_m[:], in1=b_m[:], op=ALU.mult)
-        b_c = keep.tile([P, PACK], F32, name="b_c")
-        nc.vector.tensor_scalar(out=b_c[:], in0=b_q[:], scalar1=PEDESTAL, scalar2=None, op0=ALU.subtract)
-
-        square("S", 0, 1, 0, S_COLS)
-        square("V", 0, 1, S_COLS, HALF)
-        quantise_x(0, 1)
+        def beta_c():
+            b_m = keep.tile([P, PACK], F32, name="b_m")
+            nc.vector.tensor_scalar(out=b_m[:], in0=b_sb[:], scalar1=BETA_BOUND, scalar2=None, op0=ALU.max)
+            b_q = keep.tile([P, PACK], F32, name="b_q")
+            nc.vector.tensor_tensor(out=b_q[:], in0=b_m[:], in1=b_m[:], op=ALU.mult)
+            b_out = keep.tile([P, PACK], F32, name="b_c")
+            nc.vector.tensor_scalar(out=b_out[:], in0=b_q[:], scalar1=PEDESTAL, scalar2=None, op0=ALU.subtract)
+            return b_out
 
         units = [(b, j) for b in range(BATCH) for j in range(PACK)]
         acc = {}
+        state = {"issued": 0, "read": 0}
+        quantised = set()
 
         def matmuls(u):
             b, j = units[u]
@@ -174,30 +166,72 @@ def tile_gdn_kernel(tc, inputs, beta, gamma, out):
                 )
                 acc[(u, h)] = ps
 
-        issued = 0
-        for u in range(3):
-            matmuls(u)
-            issued = u + 1
+        def pump():
+            while state["issued"] < min(len(units), state["read"] + 3):
+                b = units[state["issued"]][0]
+                if (b, 0) not in quantised or (b, 1) not in quantised:
+                    return
+                matmuls(state["issued"])
+                state["issued"] = state["issued"] + 1
+
+        def quantise(b, h):
+            quantise_x(b, h)
+            quantised.add((b, h))
+            pump()
+
+        def squares(b, h, who, part=None):
+            s = S_COLS[b]
+            if who == "V":
+                square("V", b, h, s, HALF)
+            elif part is None:
+                square("S", b, h, 0, s)
+            else:
+                square("S", b, h, part * (s // 2), (part + 1) * (s // 2))
+
+        clamp_gamma("V", 0)
+        clamp_gamma("V", 1)
+        squares(0, 0, "S")
+        finish_gamma(0, 2 * CH)
+        clamp_gamma("S", 2)
+        clamp_gamma("S", 3)
+        squares(0, 0, "V")
+        finish_gamma(2 * CH, 4 * CH)
+        quantise_gamma(0, 2 * CH)
+        quantise_gamma(2 * CH, 4 * CH)
+        b_c = beta_c()
+        squares(0, 1, "S")
+        squares(0, 1, "V")
+        quantise(0, 0)
+        squares(1, 0, "S")
+        squares(1, 0, "V")
+        quantise(0, 1)
+        squares(1, 1, "S")
+        squares(1, 1, "V")
+        quantise(1, 0)
+
+        scalar_extra = {1: (2, 0, 0), 2: (2, 0, 1), 3: (2, 1, 0), 4: (2, 1, 1)}
+        vector_square = {1: (2, 0), 4: (2, 1)}
+        vector_quantise = {0: (1, 1), 3: (2, 0), 6: (2, 1)}
 
         for u in range(len(units)):
             b, j = units[u]
-            step = u % PACK
-            limit = min(len(units), u + 4)
-            if step < 3:
-                limit = min(limit, (b + 1) * PACK)
-            while issued < limit:
-                matmuls(issued)
-                issued += 1
-
             rn = rot.tile([P, PIX], F32, tag="rn", name="rn%d" % u)
             for h in range(2):
                 nc.scalar.activation(
                     out=rn[:, h * HALF:(h + 1) * HALF], in_=acc[(u, h)][:],
                     func=ACT.Abs_reciprocal_sqrt, bias=b_c[:, j:j + 1], scale=1.0,
                 )
-            if b + 1 < BATCH and step < 2:
-                square("S", b + 1, step, 0, S_COLS)
-                square("V", b + 1, step, S_COLS, HALF)
+            state["read"] = u + 1
+            pump()
+            if u in scalar_extra:
+                nb, nh, part = scalar_extra[u]
+                squares(nb, nh, "S", part)
+            if u in vector_square:
+                nb, nh = vector_square[u]
+                squares(nb, nh, "V")
+            if u in vector_quantise:
+                nb, nh = vector_quantise[u]
+                quantise(nb, nh)
 
             o_sb = rot.tile([P, PIX], F32, tag="o", name="o%d" % u, bufs=6)
             last = u == len(units) - 1
@@ -213,6 +247,3 @@ def tile_gdn_kernel(tc, inputs, beta, gamma, out):
                 nc.vector.tensor_tensor(out=o_sb[:], in0=x_full[b][:, j, :], in1=rn[:], op=ALU.mult)
             if not last:
                 nc.sync.dma_start(out=o_dram[b][:, j, :], in_=o_sb[:])
-
-            if b + 1 < BATCH and 1 <= step < 3:
-                quantise_x(b + 1, step - 1)

@@ -17,6 +17,7 @@ BATCH = 3
 CH = 512
 PIX = 1024
 HALF = 512
+QUARTER = 256
 
 FLOPS = 2 * CH * CH * BATCH * PIX
 
@@ -24,8 +25,10 @@ PEDESTAL = 2.0 ** -36
 GAMMA_BOUND = 2.0 ** -18
 BETA_BOUND = (1e-06 + PEDESTAL) ** 0.5
 
-PINNED = True
-S_COLS = (384, 384, 320)
+S0 = 128
+S_COLS = (None, 320, 352)
+AHEAD = 3
+LAST_PIECES = ((0, 512), (512, 768), (768, 1024))
 
 
 def tile_gdn_kernel(tc, inputs, beta, gamma, out):
@@ -39,35 +42,38 @@ def tile_gdn_kernel(tc, inputs, beta, gamma, out):
         keep = ctx.enter_context(tc.tile_pool(name="keep", bufs=1))
         rot = ctx.enter_context(tc.tile_pool(name="rot", bufs=4))
         psum = ctx.enter_context(tc.psum_pool(name="psum", bufs=8))
-        if PINNED:
-            ctx.enter_context(tc.manual_schedule())
+        ctx.enter_context(tc.manual_schedule())
 
         b_sb = keep.tile([P, PACK], BF16, name="b_sb")
         nc.scalar.dma_start(out=b_sb[:], in_=b_dram)
         g_sb = []
-        x0 = []
-        for h in range(2):
-            gh = keep.tile([P, 2, CH], BF16, name="g_sb%d" % h)
-            nc.sync.dma_start(out=gh[:], in_=g_dram[:, 2 * h:2 * h + 2, :])
+        x0 = keep.tile([P, PIX // QUARTER, PACK, QUARTER], BF16, name="x0")
+
+        def load_x0(k):
+            nc.sync.dma_start(out=x0[:, k, :, :], in_=x_dram[0][:, :, k * QUARTER:(k + 1) * QUARTER])
+
+        for k in range(2):
+            gh = keep.tile([P, 2 * CH], BF16, name="g_sb%d" % k)
+            nc.sync.dma_start(out=gh[:].rearrange("m (j c) -> m j c", j=2), in_=g_dram[:, 2 * k:2 * k + 2, :])
             g_sb.append(gh)
-            xt = keep.tile([P, PACK, HALF], BF16, name="x0h%d" % h)
-            nc.sync.dma_start(out=xt[:], in_=x_dram[0][:, :, h * HALF:(h + 1) * HALF])
-            x0.append(xt)
+            load_x0(k)
+        load_x0(2)
+        load_x0(3)
         x_full = {}
         for b in range(1, BATCH):
             xt = keep.tile([P, PACK, PIX], BF16, name="x%d" % b)
             nc.sync.dma_start(out=xt[:], in_=x_dram[b])
             x_full[b] = xt
 
-        def x_half(b, h):
+        def x_cols(b, n0, n1):
             if b == 0:
-                return x0[h][:]
-            return x_full[b][:, :, h * HALF:(h + 1) * HALF]
+                k = n0 // QUARTER
+                assert n1 <= (k + 1) * QUARTER
+                return x0[:, k, :, n0 - k * QUARTER:n1 - k * QUARTER]
+            return x_full[b][:, :, n0:n1]
 
         ones = keep.tile([P, 1], F32, name="ones")
         nc.vector.memset(ones[:], 1.0)
-        negb = keep.tile([P, 1], F32, name="negb")
-        nc.vector.memset(negb[:], -GAMMA_BOUND)
         warm = keep.tile([P, 1], F32, name="warm")
         nc.scalar.activation(out=warm[:], in_=ones[:], func=ACT.Abs_reciprocal_sqrt)
         ident = keep.tile([P, P], F32, name="ident")
@@ -81,61 +87,44 @@ def tile_gdn_kernel(tc, inputs, beta, gamma, out):
                 xg[(b, h)] = keep.tile([P, HALF, PACK], BF16, name="xg%d%d" % (b, h), align_bytes=64)
                 xc[(b, h)] = keep.tile([P, HALF], U32, name="xc%d%d" % (b, h), align_bytes=64)
                 xs[(b, h)] = keep.tile([P, HALF], U8, name="xs%d%d" % (b, h), align_bytes=64)
-        g_r = keep.tile([P, PACK * CH], F32, name="g_r")
+        g_q = keep.tile([P, PACK * CH], F32, name="g_q")
         g_c = keep.tile([P, PACK * CH], BF16, name="g_c", align_bytes=64)
         g_codes = keep.tile([P, CH], U32, name="g_codes", align_bytes=64)
         g_scales = keep.tile([P, CH], U8, name="g_scales", align_bytes=64)
 
-        def square(eng, b, h, n0, n1):
-            if n1 <= n0:
-                return
-            src = x_half(b, h)[:, :, n0:n1].rearrange("p t (c i) -> p c t i", i=4)
-            dst = xg[(b, h)][:, n0:n1, :].rearrange("p (c i) t -> p c t i", i=4)
+        def square(eng, b, n0, n1):
+            h = n0 // HALF
+            src = x_cols(b, n0, n1).rearrange("p t (c i) -> p c t i", i=4)
+            dst = xg[(b, h)][:, n0 - h * HALF:n1 - h * HALF, :].rearrange("p (c i) t -> p c t i", i=4)
             if eng == "S":
                 nc.scalar.activation(out=dst, in_=src, func=ACT.Square)
             else:
                 nc.vector.tensor_tensor(out=dst, in0=src, in1=src, op=ALU.mult)
 
-        def quantise_x(b, h):
-            nc.vector.quantize_mx(
-                out=xc[(b, h)][:].bitcast(FP8X4),
-                scales=xs[(b, h)][:],
-                in_=xg[(b, h)][:].rearrange("p n t -> p (n t)"),
-            )
+        g_m = []
+        g_t = {}
 
-        g_t = []
-        for j in range(PACK):
-            g_words = (
-                g_sb[j // 2][:].rearrange("m j c -> m (j c)").bitcast(F32)
-                .rearrange("m (j q u) -> m j u q", j=2, u=2)
-            )
-            gt = psum.tile([P, HALF], F32, tag="bank", name="gt%d" % j)
-            for u in range(2):
-                nc.tensor.transpose(gt[:, u * P:(u + 1) * P], g_words[:, j % 2, u, :], ident[:])
-            g_t.append(gt)
+        def clamp_gamma(k):
+            gm = keep.tile([P, 2 * CH], BF16, name="g_m%d" % k)
+            nc.vector.tensor_scalar(out=gm[:], in0=g_sb[k][:], scalar1=GAMMA_BOUND, scalar2=None, op0=ALU.max)
+            g_m.append(gm)
+            g_words = gm[:].bitcast(F32).rearrange("m (j q u) -> m j u q", j=2, u=2)
+            for jj in range(2):
+                gt = psum.tile([P, HALF], F32, tag="bank", name="gt%d" % (2 * k + jj))
+                for u in range(2):
+                    nc.tensor.transpose(gt[:, u * P:(u + 1) * P], g_words[:, jj, u, :], ident[:])
+                g_t[2 * k + jj] = gt
 
-        def clamp_gamma(eng, j):
+        def square_gamma(j):
             src = g_t[j][:, 0:2 * P].bitcast(BF16).rearrange("q (u m e) -> q m u e", u=2, e=2)
-            dst = g_r[:, j * CH:(j + 1) * CH].rearrange("q (m u e) -> q m u e", u=2, e=2)
-            if eng == "S":
-                nc.scalar.activation(out=dst, in_=src, func=ACT.Relu, bias=negb[:, 0:1], scale=1.0)
-            else:
-                nc.vector.tensor_scalar(
-                    out=dst, in0=src, scalar1=GAMMA_BOUND, scalar2=GAMMA_BOUND, op0=ALU.max, op1=ALU.subtract
-                )
+            dst = g_q[:, j * CH:(j + 1) * CH].rearrange("q (m u e) -> q m u e", u=2, e=2)
+            nc.scalar.activation(out=dst, in_=src, func=ACT.Square)
 
         def finish_gamma(a, b):
-            nc.vector.scalar_tensor_tensor(
-                out=g_c[:, a:b], in0=g_r[:, a:b], scalar=2.0 * GAMMA_BOUND, in1=g_r[:, a:b],
-                op0=ALU.add, op1=ALU.mult,
-            )
+            nc.vector.tensor_scalar(out=g_c[:, a:b], in0=g_q[:, a:b], scalar1=PEDESTAL, scalar2=None, op0=ALU.subtract)
 
-        def quantise_gamma(a, b):
-            nc.vector.quantize_mx(
-                out=g_codes[:, a // PACK:b // PACK].bitcast(FP8X4),
-                scales=g_scales[:, a // PACK:b // PACK],
-                in_=g_c[:, a:b],
-            )
+        def quantise_gamma():
+            nc.vector.quantize_mx(out=g_codes[:].bitcast(FP8X4), scales=g_scales[:], in_=g_c[:])
 
         def beta_c():
             b_m = keep.tile([P, PACK], F32, name="b_m")
@@ -148,7 +137,7 @@ def tile_gdn_kernel(tc, inputs, beta, gamma, out):
 
         units = [(b, j) for b in range(BATCH) for j in range(PACK)]
         acc = {}
-        state = {"issued": 0, "read": 0}
+        state = {"issued": 0, "read": 0, "gamma": False}
         quantised = set()
 
         def matmuls(u):
@@ -167,7 +156,7 @@ def tile_gdn_kernel(tc, inputs, beta, gamma, out):
                 acc[(u, h)] = ps
 
         def pump():
-            while state["issued"] < min(len(units), state["read"] + 3):
+            while state["gamma"] and state["issued"] < min(len(units), state["read"] + AHEAD):
                 b = units[state["issued"]][0]
                 if (b, 0) not in quantised or (b, 1) not in quantised:
                     return
@@ -175,43 +164,46 @@ def tile_gdn_kernel(tc, inputs, beta, gamma, out):
                 state["issued"] = state["issued"] + 1
 
         def quantise(b, h):
-            quantise_x(b, h)
+            nc.vector.quantize_mx(
+                out=xc[(b, h)][:].bitcast(FP8X4),
+                scales=xs[(b, h)][:],
+                in_=xg[(b, h)][:].rearrange("p n t -> p (n t)"),
+            )
             quantised.add((b, h))
             pump()
 
-        def squares(b, h, who, part=None):
-            s = S_COLS[b]
-            if who == "V":
-                square("V", b, h, s, HALF)
-            elif part is None:
-                square("S", b, h, 0, s)
-            else:
-                square("S", b, h, part * (s // 2), (part + 1) * (s // 2))
-
-        clamp_gamma("V", 0)
-        clamp_gamma("V", 1)
-        squares(0, 0, "S")
-        finish_gamma(0, 2 * CH)
-        clamp_gamma("S", 2)
-        clamp_gamma("S", 3)
-        squares(0, 0, "V")
-        finish_gamma(2 * CH, 4 * CH)
-        quantise_gamma(0, 2 * CH)
-        quantise_gamma(2 * CH, 4 * CH)
+        s1 = S_COLS[1]
+        clamp_gamma(0)
+        square("S", 0, 0, S0)
+        square("V", 0, S0, QUARTER)
+        clamp_gamma(1)
         b_c = beta_c()
-        squares(0, 1, "S")
-        squares(0, 1, "V")
+        square_gamma(0)
+        square_gamma(1)
+        square("V", 0, QUARTER + S0, HALF)
+        finish_gamma(0, 2 * CH)
+        square_gamma(2)
+        square_gamma(3)
+        square("S", 0, QUARTER, QUARTER + S0)
+        square("V", 0, HALF + S0, HALF + QUARTER)
+        finish_gamma(2 * CH, 4 * CH)
+        square("S", 0, HALF, HALF + S0)
+        square("V", 0, HALF + QUARTER + S0, PIX)
+        quantise_gamma()
+        state["gamma"] = True
         quantise(0, 0)
-        squares(1, 0, "S")
-        squares(1, 0, "V")
+        square("S", 0, HALF + QUARTER, HALF + QUARTER + S0)
+        square("S", 1, 0, s1)
+        square("V", 1, s1, HALF)
         quantise(0, 1)
-        squares(1, 1, "S")
-        squares(1, 1, "V")
+        square("S", 1, HALF, HALF + s1)
+        square("V", 1, HALF + s1, PIX)
         quantise(1, 0)
 
-        scalar_extra = {1: (2, 0, 0), 2: (2, 0, 1), 3: (2, 1, 0), 4: (2, 1, 1)}
-        vector_square = {1: (2, 0), 4: (2, 1)}
-        vector_quantise = {0: (1, 1), 3: (2, 0), 6: (2, 1)}
+        s2 = S_COLS[2]
+        scalar_extra = {1: (0, s2 // 2), 2: (s2 // 2, s2), 3: (HALF, HALF + s2 // 2), 4: (HALF + s2 // 2, HALF + s2)}
+        vector_square = {1: (s2, HALF), 4: (HALF + s2, PIX)}
+        vector_quantise = {0: (1, 1), 3: (2, 0), 5: (2, 1)}
 
         for u in range(len(units)):
             b, j = units[u]
@@ -224,26 +216,25 @@ def tile_gdn_kernel(tc, inputs, beta, gamma, out):
             state["read"] = u + 1
             pump()
             if u in scalar_extra:
-                nb, nh, part = scalar_extra[u]
-                squares(nb, nh, "S", part)
+                square("S", 2, scalar_extra[u][0], scalar_extra[u][1])
             if u in vector_square:
-                nb, nh = vector_square[u]
-                squares(nb, nh, "V")
+                square("V", 2, vector_square[u][0], vector_square[u][1])
             if u in vector_quantise:
-                nb, nh = vector_quantise[u]
-                quantise(nb, nh)
+                quantise(vector_quantise[u][0], vector_quantise[u][1])
 
             o_sb = rot.tile([P, PIX], F32, tag="o", name="o%d" % u, bufs=6)
-            last = u == len(units) - 1
-            if b == 0 or last:
-                for h in range(2):
-                    cols = slice(h * HALF, (h + 1) * HALF)
+            if u == len(units) - 1:
+                for n0, n1 in LAST_PIECES:
                     nc.vector.tensor_tensor(
-                        out=o_sb[:, cols], in0=x_half(b, h)[:, j, :], in1=rn[:, cols], op=ALU.mult
+                        out=o_sb[:, n0:n1], in0=x_full[b][:, j, n0:n1], in1=rn[:, n0:n1], op=ALU.mult
                     )
-                    if last:
-                        nc.sync.dma_start(out=o_dram[b][:, j, cols], in_=o_sb[:, cols])
+                    nc.sync.dma_start(out=o_dram[b][:, j, n0:n1], in_=o_sb[:, n0:n1])
             else:
-                nc.vector.tensor_tensor(out=o_sb[:], in0=x_full[b][:, j, :], in1=rn[:], op=ALU.mult)
-            if not last:
+                if b == 0:
+                    nc.vector.tensor_tensor(
+                        out=o_sb[:].rearrange("p (k n) -> p k n", n=QUARTER), in0=x0[:, :, j, :],
+                        in1=rn[:].rearrange("p (k n) -> p k n", n=QUARTER), op=ALU.mult,
+                    )
+                else:
+                    nc.vector.tensor_tensor(out=o_sb[:], in0=x_full[b][:, j, :], in1=rn[:], op=ALU.mult)
                 nc.sync.dma_start(out=o_dram[b][:, j, :], in_=o_sb[:])

@@ -59,18 +59,19 @@ def tile_gdn_kernel(tc, inputs, beta, gamma, out):
             load_x0(k)
         load_x0(2)
         load_x0(3)
-        x_full = {}
-        for b in range(1, BATCH):
-            xt = keep.tile([P, PACK, PIX], BF16, name="x%d" % b)
-            nc.sync.dma_start(out=xt[:], in_=x_dram[b])
-            x_full[b] = xt
+        x1 = keep.tile([P, PIX // HALF, PACK, HALF], BF16, name="x1")
+        for k in range(PIX // HALF):
+            nc.sync.dma_start(out=x1[:, k, :, :], in_=x_dram[1][:, :, k * HALF:(k + 1) * HALF])
+        x2 = keep.tile([P, PACK, PIX], BF16, name="x2")
+        nc.sync.dma_start(out=x2[:], in_=x_dram[2])
 
         def x_cols(b, n0, n1):
-            if b == 0:
-                k = n0 // QUARTER
-                assert n1 <= (k + 1) * QUARTER
-                return x0[:, k, :, n0 - k * QUARTER:n1 - k * QUARTER]
-            return x_full[b][:, :, n0:n1]
+            if b == 2:
+                return x2[:, :, n0:n1]
+            chunked, width = ((x0, QUARTER), (x1, HALF))[b]
+            k = n0 // width
+            assert n1 <= (k + 1) * width
+            return chunked[:, k, :, n0 - k * width:n1 - k * width]
 
         ones = keep.tile([P, 1], F32, name="ones")
         nc.vector.memset(ones[:], 1.0)
@@ -180,22 +181,22 @@ def tile_gdn_kernel(tc, inputs, beta, gamma, out):
         b_c = beta_c()
         square_gamma(0)
         square_gamma(1)
+        square("S", 0, QUARTER, QUARTER + S0)
         square("V", 0, QUARTER + S0, HALF)
         finish_gamma(0, 2 * CH)
+        quantise(0, 0)
         square_gamma(2)
         square_gamma(3)
-        square("S", 0, QUARTER, QUARTER + S0)
         square("V", 0, HALF + S0, HALF + QUARTER)
         finish_gamma(2 * CH, 4 * CH)
         square("S", 0, HALF, HALF + S0)
         square("V", 0, HALF + QUARTER + S0, PIX)
         quantise_gamma()
         state["gamma"] = True
-        quantise(0, 0)
         square("S", 0, HALF + QUARTER, HALF + QUARTER + S0)
+        quantise(0, 1)
         square("S", 1, 0, s1)
         square("V", 1, s1, HALF)
-        quantise(0, 1)
         square("S", 1, HALF, HALF + s1)
         square("V", 1, HALF + s1, PIX)
         quantise(1, 0)
@@ -226,15 +227,16 @@ def tile_gdn_kernel(tc, inputs, beta, gamma, out):
             if u == len(units) - 1:
                 for n0, n1 in LAST_PIECES:
                     nc.vector.tensor_tensor(
-                        out=o_sb[:, n0:n1], in0=x_full[b][:, j, n0:n1], in1=rn[:, n0:n1], op=ALU.mult
+                        out=o_sb[:, n0:n1], in0=x2[:, j, n0:n1], in1=rn[:, n0:n1], op=ALU.mult
                     )
                     nc.sync.dma_start(out=o_dram[b][:, j, n0:n1], in_=o_sb[:, n0:n1])
             else:
-                if b == 0:
-                    nc.vector.tensor_tensor(
-                        out=o_sb[:].rearrange("p (k n) -> p k n", n=QUARTER), in0=x0[:, :, j, :],
-                        in1=rn[:].rearrange("p (k n) -> p k n", n=QUARTER), op=ALU.mult,
-                    )
+                if b == 2:
+                    nc.vector.tensor_tensor(out=o_sb[:], in0=x2[:, j, :], in1=rn[:], op=ALU.mult)
                 else:
-                    nc.vector.tensor_tensor(out=o_sb[:], in0=x_full[b][:, j, :], in1=rn[:], op=ALU.mult)
+                    chunked, width = ((x0, QUARTER), (x1, HALF))[b]
+                    nc.vector.tensor_tensor(
+                        out=o_sb[:].rearrange("p (k n) -> p k n", n=width), in0=chunked[:, :, j, :],
+                        in1=rn[:].rearrange("p (k n) -> p k n", n=width), op=ALU.mult,
+                    )
                 nc.sync.dma_start(out=o_dram[b][:, j, :], in_=o_sb[:])

@@ -26,8 +26,9 @@ GAMMA_BOUND = 2.0 ** -18
 BETA_BOUND = (1e-06 + PEDESTAL) ** 0.5
 
 S0 = 128
-S_COLS = (None, 320, 352)
-AHEAD = 3
+S_COLS = (None, 224, 352)
+AHEAD = 2
+G_PIECE = 80
 LAST_PIECES = ((0, 512), (512, 768), (768, 1024))
 
 
@@ -41,7 +42,7 @@ def tile_gdn_kernel(tc, inputs, beta, gamma, out):
     with ExitStack() as ctx:
         keep = ctx.enter_context(tc.tile_pool(name="keep", bufs=1))
         rot = ctx.enter_context(tc.tile_pool(name="rot", bufs=4))
-        psum = ctx.enter_context(tc.psum_pool(name="psum", bufs=8))
+        psum = ctx.enter_context(tc.psum_pool(name="psum", bufs=4))
         ctx.enter_context(tc.manual_schedule())
 
         b_sb = keep.tile([P, PACK], BF16, name="b_sb")
@@ -79,6 +80,8 @@ def tile_gdn_kernel(tc, inputs, beta, gamma, out):
         nc.scalar.activation(out=warm[:], in_=ones[:], func=ACT.Abs_reciprocal_sqrt)
         ident = keep.tile([P, P], F32, name="ident")
         make_identity(nc, ident[:])
+        ident_bf = keep.tile([P, P], BF16, name="ident_bf")
+        nc.vector.tensor_copy(out=ident_bf[:], in_=ident[:])
 
         xg = {}
         xc = {}
@@ -99,8 +102,23 @@ def tile_gdn_kernel(tc, inputs, beta, gamma, out):
             dst = xg[(b, h)][:, n0 - h * HALF:n1 - h * HALF, :].rearrange("p (c i) t -> p c t i", i=4)
             if eng == "S":
                 nc.scalar.activation(out=dst, in_=src, func=ACT.Square)
+            elif eng == "G":
+                nc.gpsimd.tensor_tensor(out=dst, in0=src, in1=src, op=ALU.mult)
             else:
                 nc.vector.tensor_tensor(out=dst, in0=src, in1=src, op=ALU.mult)
+
+        x_ps = {}
+
+        def numerator_to_psum(u):
+            j = u % PACK
+            for h in range(2):
+                xp = psum.tile([P, HALF], F32, tag="xp", name="xp%d_%d" % (u, h))
+                for k in range(2):
+                    nc.tensor.matmul(
+                        out=xp[:, k * QUARTER:(k + 1) * QUARTER], lhsT=ident_bf[:], rhs=x0[:, 2 * h + k, j, :],
+                        start=True, stop=True,
+                    )
+                x_ps[(u, h)] = xp
 
         g_m = []
         g_t = {}
@@ -178,6 +196,8 @@ def tile_gdn_kernel(tc, inputs, beta, gamma, out):
         square("S", 0, 0, S0)
         square("V", 0, S0, QUARTER)
         clamp_gamma(1)
+        numerator_to_psum(0)
+        numerator_to_psum(1)
         b_c = beta_c()
         square_gamma(0)
         square_gamma(1)
@@ -203,7 +223,9 @@ def tile_gdn_kernel(tc, inputs, beta, gamma, out):
 
         s2 = S_COLS[2]
         scalar_extra = {1: (0, s2 // 2), 2: (s2 // 2, s2), 3: (HALF, HALF + s2 // 2), 4: (HALF + s2 // 2, HALF + s2)}
-        vector_square = {1: (s2, HALF), 4: (HALF + s2, PIX)}
+        for h in range(2):
+            for n0 in range(h * HALF + s2, (h + 1) * HALF, G_PIECE):
+                square("G", 2, n0, n0 + G_PIECE)
         vector_quantise = {0: (1, 1), 3: (2, 0), 5: (2, 1)}
 
         for u in range(len(units)):
@@ -216,10 +238,10 @@ def tile_gdn_kernel(tc, inputs, beta, gamma, out):
                 )
             state["read"] = u + 1
             pump()
+            if 1 <= u < PACK - 1:
+                numerator_to_psum(u + 1)
             if u in scalar_extra:
                 square("S", 2, scalar_extra[u][0], scalar_extra[u][1])
-            if u in vector_square:
-                square("V", 2, vector_square[u][0], vector_square[u][1])
             if u in vector_quantise:
                 quantise(vector_quantise[u][0], vector_quantise[u][1])
 
@@ -233,10 +255,13 @@ def tile_gdn_kernel(tc, inputs, beta, gamma, out):
             else:
                 if b == 2:
                     nc.vector.tensor_tensor(out=o_sb[:], in0=x2[:, j, :], in1=rn[:], op=ALU.mult)
-                else:
-                    chunked, width = ((x0, QUARTER), (x1, HALF))[b]
+                elif b == 1:
                     nc.vector.tensor_tensor(
-                        out=o_sb[:].rearrange("p (k n) -> p k n", n=width), in0=chunked[:, :, j, :],
-                        in1=rn[:].rearrange("p (k n) -> p k n", n=width), op=ALU.mult,
+                        out=o_sb[:].rearrange("p (k n) -> p k n", n=HALF), in0=x1[:, :, j, :],
+                        in1=rn[:].rearrange("p (k n) -> p k n", n=HALF), op=ALU.mult,
                     )
+                else:
+                    for h in range(2):
+                        cols = slice(h * HALF, (h + 1) * HALF)
+                        nc.vector.tensor_tensor(out=o_sb[:, cols], in0=x_ps[(u, h)][:], in1=rn[:, cols], op=ALU.mult)
                 nc.sync.dma_start(out=o_dram[b][:, j, :], in_=o_sb[:])

@@ -28,6 +28,7 @@ BETA_BOUND = (1e-06 + PEDESTAL) ** 0.5
 S0 = 128
 S_COLS = (None, 224, 352)
 AHEAD = 2
+FINE_FROM = 5
 G_PIECE = 80
 LAST_PIECES = ((0, 512), (512, 768), (768, 1024))
 
@@ -246,10 +247,10 @@ def tile_gdn_kernel(tc, inputs, beta, gamma, out):
                 quantise(vector_quantise[u][0], vector_quantise[u][1])
 
             o_sb = rot.tile([P, PIX], F32, tag="o", name="o%d" % u, bufs=6)
-            if u == len(units) - 1:
-                for n0, n1 in LAST_PIECES:
+            if u >= FINE_FROM:
+                for n0, n1 in (LAST_PIECES if u == len(units) - 1 else ((0, 512), (512, 1024))):
                     nc.vector.tensor_tensor(
-                        out=o_sb[:, n0:n1], in0=x2[:, j, n0:n1], in1=rn[:, n0:n1], op=ALU.mult
+                        out=o_sb[:, n0:n1], in0=x_cols(b, n0, n1)[:, j, :], in1=rn[:, n0:n1], op=ALU.mult
                     )
                     nc.sync.dma_start(out=o_dram[b][:, j, n0:n1], in_=o_sb[:, n0:n1])
             else:

@@ -26,10 +26,10 @@ GAMMA_BOUND = 2.0 ** -18
 BETA_BOUND = (1e-06 + PEDESTAL) ** 0.5
 
 S0 = 128
-S_COLS = (None, 224, 352)
+S_COLS = (None, 272, 256)
 AHEAD = 2
 FINE_FROM = 5
-G_PIECE = 80
+G_PIECE = 128
 LAST_PIECES = ((0, 512), (512, 768), (768, 1024))
 
 

@@ -104,7 +104,8 @@ def tile_gdn_kernel(tc, inputs, beta, gamma, out):
             if eng == "S":
                 nc.scalar.activation(out=dst, in_=src, func=ACT.Square)
             elif eng == "G":
-                nc.gpsimd.tensor_tensor(out=dst, in0=src, in1=src, op=ALU.mult)
+                rows = x_cols(b, n0, n1).rearrange("p t n -> p n t")
+                nc.gpsimd.tensor_tensor(out=xg[(b, h)][:, n0 - h * HALF:n1 - h * HALF, :], in0=rows, in1=rows, op=ALU.mult)
             else:
                 nc.vector.tensor_tensor(out=dst, in0=src, in1=src, op=ALU.mult)
 

@@ -28,6 +28,7 @@ BETA_BOUND = (1e-06 + PEDESTAL) ** 0.5
 S0 = 128
 S_COLS = (None, 272, 256)
 AHEAD = 2
+RUN = 8
 FINE_FROM = 5
 G_PIECE = 128
 LAST_PIECES = ((0, 512), (512, 768), (768, 1024))
@@ -99,8 +100,8 @@ def tile_gdn_kernel(tc, inputs, beta, gamma, out):
 
         def square(eng, b, n0, n1):
             h = n0 // HALF
-            src = x_cols(b, n0, n1).rearrange("p t (c i) -> p c t i", i=4)
-            dst = xg[(b, h)][:, n0 - h * HALF:n1 - h * HALF, :].rearrange("p (c i) t -> p c t i", i=4)
+            src = x_cols(b, n0, n1).rearrange("p t (c i) -> p c t i", i=RUN)
+            dst = xg[(b, h)][:, n0 - h * HALF:n1 - h * HALF, :].rearrange("p (c i) t -> p c t i", i=RUN)
             if eng == "S":
                 nc.scalar.activation(out=dst, in_=src, func=ACT.Square)
             elif eng == "G":

@@ -26,10 +26,10 @@ GAMMA_BOUND = 2.0 ** -18
 BETA_BOUND = (1e-06 + PEDESTAL) ** 0.5
 
 S0 = 128
-S_COLS = (None, 272, 256)
+S_COLS = (None, 288, 256)
 AHEAD = 2
 RUN = 8
-FINE_FROM = 5
+FINE_FROM = 4
 G_PIECE = 128
 LAST_PIECES = ((0, 512), (512, 768), (768, 1024))
 
@@ -48,7 +48,6 @@ def tile_gdn_kernel(tc, inputs, beta, gamma, out):
         ctx.enter_context(tc.manual_schedule())
 
         b_sb = keep.tile([P, PACK], BF16, name="b_sb")
-        nc.scalar.dma_start(out=b_sb[:], in_=b_dram)
         g_sb = []
         x0 = keep.tile([P, PIX // QUARTER, PACK, QUARTER], BF16, name="x0")
 
@@ -60,18 +59,19 @@ def tile_gdn_kernel(tc, inputs, beta, gamma, out):
             nc.sync.dma_start(out=gh[:].rearrange("m (j c) -> m j c", j=2), in_=g_dram[:, 2 * k:2 * k + 2, :])
             g_sb.append(gh)
             load_x0(k)
+            if k == 0:
+                nc.sync.dma_start(out=b_sb[:], in_=b_dram)
         load_x0(2)
         load_x0(3)
         x1 = keep.tile([P, PIX // HALF, PACK, HALF], BF16, name="x1")
         for k in range(PIX // HALF):
             nc.sync.dma_start(out=x1[:, k, :, :], in_=x_dram[1][:, :, k * HALF:(k + 1) * HALF])
-        x2 = keep.tile([P, PACK, PIX], BF16, name="x2")
-        nc.sync.dma_start(out=x2[:], in_=x_dram[2])
+        x2 = keep.tile([P, PIX // HALF, PACK, HALF], BF16, name="x2")
+        for k in range(PIX // HALF):
+            nc.sync.dma_start(out=x2[:, k, :, :], in_=x_dram[2][:, :, k * HALF:(k + 1) * HALF])
 
         def x_cols(b, n0, n1):
-            if b == 2:
-                return x2[:, :, n0:n1]
-            chunked, width = ((x0, QUARTER), (x1, HALF))[b]
+            chunked, width = ((x0, QUARTER), (x1, HALF), (x2, HALF))[b]
             k = n0 // width
             assert n1 <= (k + 1) * width
             return chunked[:, k, :, n0 - k * width:n1 - k * width]
@@ -256,15 +256,7 @@ def tile_gdn_kernel(tc, inputs, beta, gamma, out):
                     )
                     nc.sync.dma_start(out=o_dram[b][:, j, n0:n1], in_=o_sb[:, n0:n1])
             else:
-                if b == 2:
-                    nc.vector.tensor_tensor(out=o_sb[:], in0=x2[:, j, :], in1=rn[:], op=ALU.mult)
-                elif b == 1:
-                    nc.vector.tensor_tensor(
-                        out=o_sb[:].rearrange("p (k n) -> p k n", n=HALF), in0=x1[:, :, j, :],
-                        in1=rn[:].rearrange("p (k n) -> p k n", n=HALF), op=ALU.mult,
-                    )
-                else:
-                    for h in range(2):
-                        cols = slice(h * HALF, (h + 1) * HALF)
-                        nc.vector.tensor_tensor(out=o_sb[:, cols], in0=x_ps[(u, h)][:], in1=rn[:, cols], op=ALU.mult)
+                for h in range(2):
+                    cols = slice(h * HALF, (h + 1) * HALF)
+                    nc.vector.tensor_tensor(out=o_sb[:, cols], in0=x_ps[(u, h)][:], in1=rn[:, cols], op=ALU.mult)
                 nc.sync.dma_start(out=o_dram[b][:, j, :], in_=o_sb[:])

@@ -48,33 +48,47 @@ def tile_gdn_kernel(tc, inputs, beta, gamma, out):
         ctx.enter_context(tc.manual_schedule())
 
         b_sb = keep.tile([P, PACK], BF16, name="b_sb")
-        g_sb = []
-        x0 = keep.tile([P, PIX // QUARTER, PACK, QUARTER], BF16, name="x0")
+        g_sb = keep.tile([P, PACK * CH], BF16, name="g_sb")
+        edges = [[0,128,256,512,768,1024],[0,512,1024],[0,512,1024]]
+        x_sb = []
+        x_all = {}
+        for b in range(BATCH):
+            widths = [e1 - e0 for e0, e1 in zip(edges[b][:-1], edges[b][1:])]
+            if len(set(widths)) == 1:
+                x_all[b] = keep.tile([P, len(widths), PACK, widths[0]], BF16, name="x%d" % b)
+                x_sb.append([x_all[b][:, k, :, :] for k in range(len(widths))])
+            else:
+                row = []
+                for k in range(len(widths)):
+                    xt = keep.tile([P, PACK, widths[k]], BF16, name="x%d_%d" % (b, k))
+                    row.append(xt[:])
+                x_sb.append(row)
 
-        def load_x0(k):
-            nc.sync.dma_start(out=x0[:, k, :, :], in_=x_dram[0][:, :, k * QUARTER:(k + 1) * QUARTER])
+        def load_x(b, k):
+            nc.sync.dma_start(out=x_sb[b][k], in_=x_dram[b][:, :, edges[b][k]:edges[b][k + 1]])
 
-        for k in range(2):
-            gh = keep.tile([P, 2 * CH], BF16, name="g_sb%d" % k)
-            nc.sync.dma_start(out=gh[:].rearrange("m (j c) -> m j c", j=2), in_=g_dram[:, 2 * k:2 * k + 2, :])
-            g_sb.append(gh)
-            load_x0(k)
-            if k == 0:
-                nc.sync.dma_start(out=b_sb[:], in_=b_dram)
-        load_x0(2)
-        load_x0(3)
-        x1 = keep.tile([P, PIX // HALF, PACK, HALF], BF16, name="x1")
-        for k in range(PIX // HALF):
-            nc.sync.dma_start(out=x1[:, k, :, :], in_=x_dram[1][:, :, k * HALF:(k + 1) * HALF])
-        x2 = keep.tile([P, PIX // HALF, PACK, HALF], BF16, name="x2")
-        for k in range(PIX // HALF):
-            nc.sync.dma_start(out=x2[:, k, :, :], in_=x_dram[2][:, :, k * HALF:(k + 1) * HALF])
+        def load_g(j0, j1):
+            nc.sync.dma_start(out=g_sb[:, j0 * CH:j1 * CH].rearrange("m (j c) -> m j c", j=j1 - j0), in_=g_dram[:, j0:j1, :])
+
+        load_g(0, 1)
+        load_x(0, 0)
+        load_g(1, 2)
+        nc.sync.dma_start(out=b_sb[:], in_=b_dram)
+        load_x(0, 1)
+        load_g(2, 4)
+        load_x(0, 2)
+        load_x(0, 3)
+        load_x(0, 4)
+        load_x(1, 0)
+        load_x(1, 1)
+        load_x(2, 0)
+        load_x(2, 1)
 
         def x_cols(b, n0, n1):
-            chunked, width = ((x0, QUARTER), (x1, HALF), (x2, HALF))[b]
-            k = n0 // width
-            assert n1 <= (k + 1) * width
-            return chunked[:, k, :, n0 - k * width:n1 - k * width]
+            for k in range(len(edges[b]) - 1):
+                if edges[b][k] <= n0 and n1 <= edges[b][k + 1]:
+                    return x_sb[b][k][:, :, n0 - edges[b][k]:n1 - edges[b][k]]
+            raise ValueError("columns cross a load")
 
         ones = keep.tile([P, 1], F32, name="ones")
         nc.vector.memset(ones[:], 1.0)
@@ -112,30 +126,30 @@ def tile_gdn_kernel(tc, inputs, beta, gamma, out):
 
         x_ps = {}
 
-        def numerator_to_psum(u):
-            j = u % PACK
-            for h in range(2):
+        def numerator_to_psum(u, halves=(0, 1)):
+            b, j = u // PACK, u % PACK
+            for h in halves:
                 xp = psum.tile([P, HALF], F32, tag="xp", name="xp%d_%d" % (u, h))
-                for k in range(2):
-                    nc.tensor.matmul(
-                        out=xp[:, k * QUARTER:(k + 1) * QUARTER], lhsT=ident_bf[:], rhs=x0[:, 2 * h + k, j, :],
-                        start=True, stop=True,
-                    )
+                for n0, n1 in zip(edges[b][:-1], edges[b][1:]):
+                    if h * HALF <= n0 < (h + 1) * HALF:
+                        nc.tensor.matmul(
+                            out=xp[:, n0 - h * HALF:n1 - h * HALF], lhsT=ident_bf[:], rhs=x_cols(b, n0, n1)[:, j, :],
+                            start=True, stop=True,
+                        )
                 x_ps[(u, h)] = xp
 
-        g_m = []
         g_t = {}
 
-        def clamp_gamma(k):
-            gm = keep.tile([P, 2 * CH], BF16, name="g_m%d" % k)
-            nc.vector.tensor_scalar(out=gm[:], in0=g_sb[k][:], scalar1=GAMMA_BOUND, scalar2=None, op0=ALU.max)
-            g_m.append(gm)
-            g_words = gm[:].bitcast(F32).rearrange("m (j q u) -> m j u q", j=2, u=2)
-            for jj in range(2):
-                gt = psum.tile([P, HALF], F32, tag="bank", name="gt%d" % (2 * k + jj))
+        g_cl = keep.tile([P, PACK * CH], BF16, name="g_cl")
+
+        def clamp_gamma(j0, j1):
+            nc.vector.tensor_scalar(out=g_cl[:, j0 * CH:j1 * CH], in0=g_sb[:, j0 * CH:j1 * CH], scalar1=GAMMA_BOUND, scalar2=None, op0=ALU.max)
+            g_words = g_cl[:].bitcast(F32).rearrange("m (j q u) -> m j u q", j=PACK, u=2)
+            for j in range(j0, j1):
+                gt = psum.tile([P, HALF], F32, tag="bank", name="gt%d" % j)
                 for u in range(2):
-                    nc.tensor.transpose(gt[:, u * P:(u + 1) * P], g_words[:, jj, u, :], ident[:])
-                g_t[2 * k + jj] = gt
+                    nc.tensor.transpose(gt[:, u * P:(u + 1) * P], g_words[:, j, u, :], ident[:])
+                g_t[j] = gt
 
         def square_gamma(j):
             src = g_t[j][:, 0:2 * P].bitcast(BF16).rearrange("q (u m e) -> q m u e", u=2, e=2)
@@ -194,44 +208,7 @@ def tile_gdn_kernel(tc, inputs, beta, gamma, out):
             quantised.add((b, h))
             pump()
 
-        s1 = S_COLS[1]
-        clamp_gamma(0)
-        square("S", 0, 0, S0)
-        square("V", 0, S0, QUARTER)
-        clamp_gamma(1)
-        numerator_to_psum(0)
-        numerator_to_psum(1)
-        b_c = beta_c()
-        square_gamma(0)
-        square_gamma(1)
-        square("S", 0, QUARTER, QUARTER + S0)
-        square("V", 0, QUARTER + S0, HALF)
-        finish_gamma(0, 2 * CH)
-        quantise(0, 0)
-        square_gamma(2)
-        square_gamma(3)
-        square("V", 0, HALF + S0, HALF + QUARTER)
-        finish_gamma(2 * CH, 4 * CH)
-        square("S", 0, HALF, HALF + S0)
-        square("V", 0, HALF + QUARTER + S0, PIX)
-        quantise_gamma()
-        state["gamma"] = True
-        square("S", 0, HALF + QUARTER, HALF + QUARTER + S0)
-        quantise(0, 1)
-        square("S", 1, 0, s1)
-        square("V", 1, s1, HALF)
-        square("S", 1, HALF, HALF + s1)
-        square("V", 1, HALF + s1, PIX)
-        quantise(1, 0)
-
-        s2 = S_COLS[2]
-        scalar_extra = {1: (0, s2 // 2), 2: (s2 // 2, s2), 3: (HALF, HALF + s2 // 2), 4: (HALF + s2 // 2, HALF + s2)}
-        for h in range(2):
-            for n0 in range(h * HALF + s2, (h + 1) * HALF, G_PIECE):
-                square("G", 2, n0, n0 + G_PIECE)
-        vector_quantise = {0: (1, 1), 3: (2, 0), 5: (2, 1)}
-
-        for u in range(len(units)):
+        def read(u):
             b, j = units[u]
             rn = rot.tile([P, PIX], F32, tag="rn", name="rn%d" % u)
             for h in range(2):
@@ -239,24 +216,95 @@ def tile_gdn_kernel(tc, inputs, beta, gamma, out):
                     out=rn[:, h * HALF:(h + 1) * HALF], in_=acc[(u, h)][:],
                     func=ACT.Abs_reciprocal_sqrt, bias=b_c[:, j:j + 1], scale=1.0,
                 )
+            rns[u] = rn
             state["read"] = u + 1
             pump()
             if 1 <= u < PACK - 1:
                 numerator_to_psum(u + 1)
-            if u in scalar_extra:
-                square("S", 2, scalar_extra[u][0], scalar_extra[u][1])
-            if u in vector_quantise:
-                quantise(vector_quantise[u][0], vector_quantise[u][1])
+            if u == 3:
+                numerator_to_psum(4, (0,))
 
+        def finish(u):
+            b, j = units[u]
+            rn = rns[u]
             o_sb = rot.tile([P, PIX], F32, tag="o", name="o%d" % u, bufs=6)
-            if u >= FINE_FROM:
-                for n0, n1 in (LAST_PIECES if u == len(units) - 1 else ((0, 512), (512, 1024))):
-                    nc.vector.tensor_tensor(
-                        out=o_sb[:, n0:n1], in0=x_cols(b, n0, n1)[:, j, :], in1=rn[:, n0:n1], op=ALU.mult
-                    )
+            for n0, n1 in (LAST_PIECES if u == len(units) - 1 else ((0, 512), (512, 1024))):
+                num = x_ps[(u, n0 // HALF)][:, n0 % HALF:n0 % HALF + n1 - n0] if (u, n0 // HALF) in x_ps else x_cols(b, n0, n1)[:, j, :]
+                nc.vector.tensor_tensor(out=o_sb[:, n0:n1], in0=num, in1=rn[:, n0:n1], op=ALU.mult)
+                if u >= FINE_FROM:
                     nc.sync.dma_start(out=o_dram[b][:, j, n0:n1], in_=o_sb[:, n0:n1])
-            else:
-                for h in range(2):
-                    cols = slice(h * HALF, (h + 1) * HALF)
-                    nc.vector.tensor_tensor(out=o_sb[:, cols], in0=x_ps[(u, h)][:], in1=rn[:, cols], op=ALU.mult)
+            if u < FINE_FROM:
                 nc.sync.dma_start(out=o_dram[b][:, j, :], in_=o_sb[:])
+
+        rns = {}
+        clamp_gamma(0, 1)
+        square("S", 0, 0, 128)
+        clamp_gamma(1, 2)
+        b_m = keep.tile([P, PACK], F32, name="b_m")
+        nc.vector.tensor_scalar(out=b_m[:], in0=b_sb[:], scalar1=BETA_BOUND, scalar2=None, op0=ALU.max)
+        square("V", 0, 128, 256)
+        clamp_gamma(2, 4)
+        b_q = keep.tile([P, PACK], F32, name="b_q")
+        nc.vector.tensor_tensor(out=b_q[:], in0=b_m[:], in1=b_m[:], op=ALU.mult)
+        numerator_to_psum(0)
+        numerator_to_psum(1)
+        square_gamma(0)
+        square_gamma(1)
+        square("S", 0, 256, 384)
+        square("V", 0, 384, 512)
+        b_c = keep.tile([P, PACK], F32, name="b_c")
+        nc.vector.tensor_scalar(out=b_c[:], in0=b_q[:], scalar1=PEDESTAL, scalar2=None, op0=ALU.subtract)
+        finish_gamma(0 * CH, 2 * CH)
+        quantise(0, 0)
+        square_gamma(2)
+        square_gamma(3)
+        square("V", 0, 640, 768)
+        finish_gamma(2 * CH, 4 * CH)
+        square("S", 0, 512, 640)
+        square("V", 0, 896, 1024)
+        quantise_gamma()
+        state["gamma"] = True
+        square("S", 0, 768, 896)
+        quantise(0, 1)
+        square("S", 1, 0, 288)
+        square("V", 1, 288, 512)
+        square("S", 1, 512, 800)
+        square("V", 1, 800, 1024)
+        quantise(1, 0)
+        read(0)
+        square("G", 2, 256, 344)
+        square("G", 2, 344, 424)
+        square("G", 2, 424, 512)
+        square("G", 2, 768, 856)
+        square("G", 2, 856, 936)
+        square("G", 2, 936, 1024)
+        quantise(1, 1)
+        finish(0)
+        read(1)
+        square("S", 2, 0, 128)
+        finish(1)
+        read(2)
+        square("S", 2, 128, 256)
+        finish(2)
+        read(3)
+        square("S", 2, 512, 640)
+        quantise(2, 0)
+        finish(3)
+        read(4)
+        square("S", 2, 640, 768)
+        finish(4)
+        read(5)
+        quantise(2, 1)
+        finish(5)
+        read(6)
+        finish(6)
+        read(7)
+        finish(7)
+        read(8)
+        finish(8)
+        read(9)
+        finish(9)
+        read(10)
+        finish(10)
+        read(11)
+        finish(11)

@@ -49,7 +49,7 @@ def tile_gdn_kernel(tc, inputs, beta, gamma, out):
 
         b_sb = keep.tile([P, PACK], BF16, name="b_sb")
         g_sb = keep.tile([P, PACK * CH], BF16, name="g_sb")
-        edges = [[0,128,256,512,768,1024],[0,512,1024],[0,512,1024]]
+        edges = [[0,256,512,768,1024],[0,512,1024],[0,1024]]
         x_sb = []
         x_all = {}
         for b in range(BATCH):
@@ -74,15 +74,13 @@ def tile_gdn_kernel(tc, inputs, beta, gamma, out):
         load_x(0, 0)
         load_g(1, 2)
         nc.sync.dma_start(out=b_sb[:], in_=b_dram)
-        load_x(0, 1)
         load_g(2, 4)
+        load_x(0, 1)
         load_x(0, 2)
         load_x(0, 3)
-        load_x(0, 4)
         load_x(1, 0)
         load_x(1, 1)
         load_x(2, 0)
-        load_x(2, 1)
 
         def x_cols(b, n0, n1):
             for k in range(len(edges[b]) - 1):
@@ -240,36 +238,37 @@ def tile_gdn_kernel(tc, inputs, beta, gamma, out):
         clamp_gamma(0, 1)
         square("S", 0, 0, 128)
         clamp_gamma(1, 2)
+        square("V", 0, 128, 256)
+        square_gamma(0)
         b_m = keep.tile([P, PACK], F32, name="b_m")
         nc.vector.tensor_scalar(out=b_m[:], in0=b_sb[:], scalar1=BETA_BOUND, scalar2=None, op0=ALU.max)
-        square("V", 0, 128, 256)
         clamp_gamma(2, 4)
+        square_gamma(1)
         b_q = keep.tile([P, PACK], F32, name="b_q")
         nc.vector.tensor_tensor(out=b_q[:], in0=b_m[:], in1=b_m[:], op=ALU.mult)
-        numerator_to_psum(0)
-        numerator_to_psum(1)
-        square_gamma(0)
-        square_gamma(1)
+        finish_gamma(0 * CH, 1 * CH)
         square("S", 0, 256, 384)
         square("V", 0, 384, 512)
         b_c = keep.tile([P, PACK], F32, name="b_c")
         nc.vector.tensor_scalar(out=b_c[:], in0=b_q[:], scalar1=PEDESTAL, scalar2=None, op0=ALU.subtract)
-        finish_gamma(0 * CH, 2 * CH)
-        quantise(0, 0)
+        finish_gamma(1 * CH, 2 * CH)
+        numerator_to_psum(0)
+        numerator_to_psum(1)
         square_gamma(2)
+        quantise(0, 0)
         square_gamma(3)
         square("V", 0, 640, 768)
-        finish_gamma(2 * CH, 4 * CH)
         square("S", 0, 512, 640)
+        finish_gamma(2 * CH, 4 * CH)
         square("V", 0, 896, 1024)
         quantise_gamma()
         state["gamma"] = True
         square("S", 0, 768, 896)
         quantise(0, 1)
-        square("S", 1, 0, 288)
-        square("V", 1, 288, 512)
-        square("S", 1, 512, 800)
-        square("V", 1, 800, 1024)
+        square("S", 1, 0, 256)
+        square("V", 1, 256, 512)
+        square("S", 1, 512, 768)
+        square("V", 1, 768, 1024)
         quantise(1, 0)
         read(0)
         square("G", 2, 256, 344)

@@ -141,8 +141,13 @@ def tile_gdn_kernel(tc, inputs, beta, gamma, out):
         g_cl = keep.tile([P, PACK * CH], BF16, name="g_cl")
 
         def clamp_gamma(j0, j1):
-            nc.vector.tensor_scalar(out=g_cl[:, j0 * CH:j1 * CH], in0=g_sb[:, j0 * CH:j1 * CH], scalar1=GAMMA_BOUND, scalar2=None, op0=ALU.max)
-            g_words = g_cl[:].bitcast(F32).rearrange("m (j q u) -> m j u q", j=PACK, u=2)
+            for j in range(j0, j1):
+                nc.vector.tensor_scalar(
+                    out=g_cl[:, j * CH:(j + 1) * CH].rearrange("m (u q e) -> m u q e", u=2, e=2),
+                    in0=g_sb[:, j * CH:(j + 1) * CH].rearrange("m (q u e) -> m u q e", u=2, e=2),
+                    scalar1=GAMMA_BOUND, scalar2=None, op0=ALU.max,
+                )
+            g_words = g_cl[:].bitcast(F32).rearrange("m (j u q) -> m j u q", j=PACK, u=2)
             for j in range(j0, j1):
                 gt = psum.tile([P, HALF], F32, tag="bank", name="gt%d" % j)
                 for u in range(2):

@@ -73,11 +73,11 @@ def tile_gdn_kernel(tc, inputs, beta, gamma, out):
         load_g(0, 1)
         load_x(0, 0)
         load_g(1, 2)
-        nc.sync.dma_start(out=b_sb[:], in_=b_dram)
         load_g(2, 4)
         load_x(0, 1)
         load_x(0, 2)
         load_x(0, 3)
+        nc.sync.dma_start(out=b_sb[:], in_=b_dram)
         load_x(1, 0)
         load_x(1, 1)
         load_x(2, 0)
@@ -245,17 +245,11 @@ def tile_gdn_kernel(tc, inputs, beta, gamma, out):
         clamp_gamma(1, 2)
         square("V", 0, 128, 256)
         square_gamma(0)
-        b_m = keep.tile([P, PACK], F32, name="b_m")
-        nc.vector.tensor_scalar(out=b_m[:], in0=b_sb[:], scalar1=BETA_BOUND, scalar2=None, op0=ALU.max)
         clamp_gamma(2, 4)
         square_gamma(1)
-        b_q = keep.tile([P, PACK], F32, name="b_q")
-        nc.vector.tensor_tensor(out=b_q[:], in0=b_m[:], in1=b_m[:], op=ALU.mult)
         finish_gamma(0 * CH, 1 * CH)
         square("S", 0, 256, 384)
         square("V", 0, 384, 512)
-        b_c = keep.tile([P, PACK], F32, name="b_c")
-        nc.vector.tensor_scalar(out=b_c[:], in0=b_q[:], scalar1=PEDESTAL, scalar2=None, op0=ALU.subtract)
         finish_gamma(1 * CH, 2 * CH)
         numerator_to_psum(0)
         numerator_to_psum(1)
@@ -265,10 +259,16 @@ def tile_gdn_kernel(tc, inputs, beta, gamma, out):
         square("V", 0, 640, 768)
         square("S", 0, 512, 640)
         finish_gamma(2 * CH, 4 * CH)
+        b_m = keep.tile([P, PACK], F32, name="b_m")
+        nc.vector.tensor_scalar(out=b_m[:], in0=b_sb[:], scalar1=BETA_BOUND, scalar2=None, op0=ALU.max)
         square("V", 0, 896, 1024)
+        b_q = keep.tile([P, PACK], F32, name="b_q")
+        nc.vector.tensor_tensor(out=b_q[:], in0=b_m[:], in1=b_m[:], op=ALU.mult)
         quantise_gamma()
         state["gamma"] = True
         square("S", 0, 768, 896)
+        b_c = keep.tile([P, PACK], F32, name="b_c")
+        nc.vector.tensor_scalar(out=b_c[:], in0=b_q[:], scalar1=PEDESTAL, scalar2=None, op0=ALU.subtract)
         quantise(0, 1)
         square("S", 1, 0, 256)
         square("V", 1, 256, 512)

@@ -49,7 +49,7 @@ def tile_gdn_kernel(tc, inputs, beta, gamma, out):
 
         b_sb = keep.tile([P, PACK], BF16, name="b_sb")
         g_sb = keep.tile([P, PACK * CH], BF16, name="g_sb")
-        edges = [[0,256,512,768,1024],[0,512,1024],[0,1024]]
+        edges = [[0,256,512,1024],[0,512,1024],[0,512,1024]]
         x_sb = []
         x_all = {}
         for b in range(BATCH):
@@ -76,11 +76,11 @@ def tile_gdn_kernel(tc, inputs, beta, gamma, out):
         load_g(2, 4)
         load_x(0, 1)
         load_x(0, 2)
-        load_x(0, 3)
         nc.sync.dma_start(out=b_sb[:], in_=b_dram)
         load_x(1, 0)
         load_x(1, 1)
         load_x(2, 0)
+        load_x(2, 1)
 
         def x_cols(b, n0, n1):
             for k in range(len(edges[b]) - 1):
@@ -270,10 +270,10 @@ def tile_gdn_kernel(tc, inputs, beta, gamma, out):
         b_c = keep.tile([P, PACK], F32, name="b_c")
         nc.vector.tensor_scalar(out=b_c[:], in0=b_q[:], scalar1=PEDESTAL, scalar2=None, op0=ALU.subtract)
         quantise(0, 1)
-        square("S", 1, 0, 256)
-        square("V", 1, 256, 512)
-        square("S", 1, 512, 768)
-        square("V", 1, 768, 1024)
+        square("S", 1, 0, 272)
+        square("V", 1, 272, 512)
+        square("S", 1, 512, 784)
+        square("V", 1, 784, 1024)
         quantise(1, 0)
         read(0)
         square("G", 2, 256, 344)

from contextlib import ExitStack

import concourse.mybir as mybir
from concourse.masks import make_identity

F32 = mybir.dt.float32
BF16 = mybir.dt.bfloat16
U32 = mybir.dt.uint32
U8 = mybir.dt.uint8
FP8X4 = mybir.dt.float8_e4m3fn_x4
ALU = mybir.AluOpType
ACT = mybir.ActivationFunctionType

P = 128
PACK = 4
BATCH = 3
CH = 512
PIX = 1024
HALF = 512
QUARTER = 256

FLOPS = 2 * CH * CH * BATCH * PIX

PEDESTAL = 2.0 ** -36
GAMMA_BOUND = 2.0 ** -18
BETA_BOUND = (1e-06 + PEDESTAL) ** 0.5

S0 = 128
S_COLS = (None, 288, 256)
AHEAD = 2
RUN = 8
FINE_FROM = 4
G_PIECE = 128
LAST_PIECES = ((0, 512), (512, 768), (768, 1024))


def tile_gdn_kernel(tc, inputs, beta, gamma, out):
    nc = tc.nc
    x_dram = inputs.rearrange("b (p j) h w -> b p j (h w)", j=PACK)
    o_dram = out.rearrange("b (p j) h w -> b p j (h w)", j=PACK)
    g_dram = gamma.rearrange("(m j) c -> m j c", j=PACK)
    b_dram = beta.rearrange("(p j) -> p j", j=PACK)

    with ExitStack() as ctx:
        keep = ctx.enter_context(tc.tile_pool(name="keep", bufs=1))
        rot = ctx.enter_context(tc.tile_pool(name="rot", bufs=4))
        psum = ctx.enter_context(tc.psum_pool(name="psum", bufs=4))
        ctx.enter_context(tc.manual_schedule())

        b_sb = keep.tile([P, PACK], BF16, name="b_sb")
        g_sb = keep.tile([P, PACK * CH], BF16, name="g_sb")
        edges = [[0,256,512,1024],[0,512,1024],[0,512,1024]]
        x_sb = []
        x_all = {}
        for b in range(BATCH):
            widths = [e1 - e0 for e0, e1 in zip(edges[b][:-1], edges[b][1:])]
            if len(set(widths)) == 1:
                x_all[b] = keep.tile([P, len(widths), PACK, widths[0]], BF16, name="x%d" % b)
                x_sb.append([x_all[b][:, k, :, :] for k in range(len(widths))])
            else:
                row = []
                for k in range(len(widths)):
                    xt = keep.tile([P, PACK, widths[k]], BF16, name="x%d_%d" % (b, k))
                    row.append(xt[:])
                x_sb.append(row)

        def load_x(b, k):
            nc.sync.dma_start(out=x_sb[b][k], in_=x_dram[b][:, :, edges[b][k]:edges[b][k + 1]])

        def load_g(j0, j1):
            nc.sync.dma_start(out=g_sb[:, j0 * CH:j1 * CH].rearrange("m (j c) -> m j c", j=j1 - j0), in_=g_dram[:, j0:j1, :])

        load_g(0, 1)
        load_x(0, 0)
        load_g(1, 2)
        load_g(2, 4)
        load_x(0, 1)
        load_x(0, 2)
        nc.sync.dma_start(out=b_sb[:], in_=b_dram)
        load_x(1, 0)
        load_x(1, 1)
        load_x(2, 0)
        load_x(2, 1)

        def x_cols(b, n0, n1):
            for k in range(len(edges[b]) - 1):
                if edges[b][k] <= n0 and n1 <= edges[b][k + 1]:
                    return x_sb[b][k][:, :, n0 - edges[b][k]:n1 - edges[b][k]]
            raise ValueError("columns cross a load")

        ones = keep.tile([P, 1], F32, name="ones")
        nc.vector.memset(ones[:], 1.0)
        warm = keep.tile([P, 1], F32, name="warm")
        nc.scalar.activation(out=warm[:], in_=ones[:], func=ACT.Abs_reciprocal_sqrt)
        ident = keep.tile([P, P], F32, name="ident")
        make_identity(nc, ident[:])
        ident_bf = keep.tile([P, P], BF16, name="ident_bf")
        nc.vector.tensor_copy(out=ident_bf[:], in_=ident[:])

        xg = {}
        xc = {}
        xs = {}
        for b in range(BATCH):
            for h in range(2):
                xg[(b, h)] = keep.tile([P, HALF, PACK], BF16, name="xg%d%d" % (b, h), align_bytes=64)
                xc[(b, h)] = keep.tile([P, HALF], U32, name="xc%d%d" % (b, h), align_bytes=64)
                xs[(b, h)] = keep.tile([P, HALF], U8, name="xs%d%d" % (b, h), align_bytes=64)
        g_q = keep.tile([P, PACK * CH], F32, name="g_q")
        g_c = keep.tile([P, PACK * CH], BF16, name="g_c", align_bytes=64)
        g_codes = keep.tile([P, CH], U32, name="g_codes", align_bytes=64)
        g_scales = keep.tile([P, CH], U8, name="g_scales", align_bytes=64)

        def square(eng, b, n0, n1):
            h = n0 // HALF
            src = x_cols(b, n0, n1).rearrange("p t (c i) -> p c t i", i=RUN)
            dst = xg[(b, h)][:, n0 - h * HALF:n1 - h * HALF, :].rearrange("p (c i) t -> p c t i", i=RUN)
            if eng == "S":
                nc.scalar.activation(out=dst, in_=src, func=ACT.Square)
            elif eng == "G":
                rows = x_cols(b, n0, n1).rearrange("p t n -> p n t")
                nc.gpsimd.tensor_tensor(out=xg[(b, h)][:, n0 - h * HALF:n1 - h * HALF, :], in0=rows, in1=rows, op=ALU.mult)
            else:
                nc.vector.tensor_tensor(out=dst, in0=src, in1=src, op=ALU.mult)

        x_ps = {}

        def numerator_to_psum(u, halves=(0, 1)):
            b, j = u // PACK, u % PACK
            for h in halves:
                xp = psum.tile([P, HALF], F32, tag="xp", name="xp%d_%d" % (u, h))
                for n0, n1 in zip(edges[b][:-1], edges[b][1:]):
                    if h * HALF <= n0 < (h + 1) * HALF:
                        nc.tensor.matmul(
                            out=xp[:, n0 - h * HALF:n1 - h * HALF], lhsT=ident_bf[:], rhs=x_cols(b, n0, n1)[:, j, :],
                            start=True, stop=True,
                        )
                x_ps[(u, h)] = xp

        g_t = {}

        g_cl = keep.tile([P, PACK * CH], BF16, name="g_cl")

        def clamp_gamma(j0, j1):
            for j in range(j0, j1):
                nc.vector.tensor_scalar(
                    out=g_cl[:, j * CH:(j + 1) * CH].rearrange("m (u q e) -> m u q e", u=2, e=2),
                    in0=g_sb[:, j * CH:(j + 1) * CH].rearrange("m (q u e) -> m u q e", u=2, e=2),
                    scalar1=GAMMA_BOUND, scalar2=None, op0=ALU.max,
                )
            g_words = g_cl[:].bitcast(F32).rearrange("m (j u q) -> m j u q", j=PACK, u=2)
            for j in range(j0, j1):
                gt = psum.tile([P, HALF], F32, tag="bank", name="gt%d" % j)
                for u in range(2):
                    nc.tensor.transpose(gt[:, u * P:(u + 1) * P], g_words[:, j, u, :], ident[:])
                g_t[j] = gt

        def square_gamma(j):
            src = g_t[j][:, 0:2 * P].bitcast(BF16).rearrange("q (u m e) -> q m u e", u=2, e=2)
            dst = g_q[:, j * CH:(j + 1) * CH].rearrange("q (m u e) -> q m u e", u=2, e=2)
            nc.scalar.activation(out=dst, in_=src, func=ACT.Square)

        def finish_gamma(a, b):
            nc.vector.tensor_scalar(out=g_c[:, a:b], in0=g_q[:, a:b], scalar1=PEDESTAL, scalar2=None, op0=ALU.subtract)

        def quantise_gamma():
            nc.vector.quantize_mx(out=g_codes[:].bitcast(FP8X4), scales=g_scales[:], in_=g_c[:])

        def beta_c():
            b_m = keep.tile([P, PACK], F32, name="b_m")
            nc.vector.tensor_scalar(out=b_m[:], in0=b_sb[:], scalar1=BETA_BOUND, scalar2=None, op0=ALU.max)
            b_q = keep.tile([P, PACK], F32, name="b_q")
            nc.vector.tensor_tensor(out=b_q[:], in0=b_m[:], in1=b_m[:], op=ALU.mult)
            b_out = keep.tile([P, PACK], F32, name="b_c")
            nc.vector.tensor_scalar(out=b_out[:], in0=b_q[:], scalar1=PEDESTAL, scalar2=None, op0=ALU.subtract)
            return b_out

        units = [(b, j) for b in range(BATCH) for j in range(PACK)]
        acc = {}
        state = {"issued": 0, "read": 0, "gamma": False}
        quantised = set()

        def matmuls(u):
            b, j = units[u]
            for h in range(2):
                ps = psum.tile([P, HALF], F32, tag="bank", name="acc%d_%d" % (u, h))
                nc.tensor.matmul_mx(
                    out=ps[:],
                    lhsT=g_codes[:, j * P:(j + 1) * P].bitcast(FP8X4),
                    lhsT_scale=g_scales[:, j * P:(j + 1) * P],
                    rhs=xc[(b, h)][:].bitcast(FP8X4),
                    rhs_scale=xs[(b, h)][:],
                    start=True,
                    stop=True,
                )
                acc[(u, h)] = ps

        def pump():
            while state["gamma"] and state["issued"] < min(len(units), state["read"] + AHEAD):
                b = units[state["issued"]][0]
                if (b, 0) not in quantised or (b, 1) not in quantised:
                    return
                matmuls(state["issued"])
                state["issued"] = state["issued"] + 1

        def quantise(b, h):
            nc.vector.quantize_mx(
                out=xc[(b, h)][:].bitcast(FP8X4),
                scales=xs[(b, h)][:],
                in_=xg[(b, h)][:].rearrange("p n t -> p (n t)"),
            )
            quantised.add((b, h))
            pump()

        def read(u):
            b, j = units[u]
            rn = rot.tile([P, PIX], F32, tag="rn", name="rn%d" % u)
            for h in range(2):
                nc.scalar.activation(
                    out=rn[:, h * HALF:(h + 1) * HALF], in_=acc[(u, h)][:],
                    func=ACT.Abs_reciprocal_sqrt, bias=b_c[:, j:j + 1], scale=1.0,
                )
            rns[u] = rn
            state["read"] = u + 1
            pump()
            if 1 <= u < PACK - 1:
                numerator_to_psum(u + 1)
            if u == 3:
                numerator_to_psum(4, (0,))

        def finish(u):
            b, j = units[u]
            rn = rns[u]
            o_sb = rot.tile([P, PIX], F32, tag="o", name="o%d" % u, bufs=6)
            for n0, n1 in (LAST_PIECES if u == len(units) - 1 else ((0, 512), (512, 1024))):
                num = x_ps[(u, n0 // HALF)][:, n0 % HALF:n0 % HALF + n1 - n0] if (u, n0 // HALF) in x_ps else x_cols(b, n0, n1)[:, j, :]
                nc.vector.tensor_tensor(out=o_sb[:, n0:n1], in0=num, in1=rn[:, n0:n1], op=ALU.mult)
                if u >= FINE_FROM:
                    nc.sync.dma_start(out=o_dram[b][:, j, n0:n1], in_=o_sb[:, n0:n1])
            if u < FINE_FROM:
                nc.sync.dma_start(out=o_dram[b][:, j, :], in_=o_sb[:])

        rns = {}
        clamp_gamma(0, 1)
        square("S", 0, 0, 128)
        clamp_gamma(1, 2)
        square("V", 0, 128, 256)
        square_gamma(0)
        clamp_gamma(2, 4)
        square_gamma(1)
        finish_gamma(0 * CH, 1 * CH)
        square("S", 0, 256, 384)
        square("V", 0, 384, 512)
        finish_gamma(1 * CH, 2 * CH)
        numerator_to_psum(0)
        numerator_to_psum(1)
        square_gamma(2)
        quantise(0, 0)
        square_gamma(3)
        square("V", 0, 640, 768)
        square("S", 0, 512, 640)
        finish_gamma(2 * CH, 4 * CH)
        b_m = keep.tile([P, PACK], F32, name="b_m")
        nc.vector.tensor_scalar(out=b_m[:], in0=b_sb[:], scalar1=BETA_BOUND, scalar2=None, op0=ALU.max)
        square("V", 0, 896, 1024)
        b_q = keep.tile([P, PACK], F32, name="b_q")
        nc.vector.tensor_tensor(out=b_q[:], in0=b_m[:], in1=b_m[:], op=ALU.mult)
        quantise_gamma()
        state["gamma"] = True
        square("S", 0, 768, 896)
        b_c = keep.tile([P, PACK], F32, name="b_c")
        nc.vector.tensor_scalar(out=b_c[:], in0=b_q[:], scalar1=PEDESTAL, scalar2=None, op0=ALU.subtract)
        quantise(0, 1)
        square("S", 1, 0, 272)
        square("V", 1, 272, 512)
        square("S", 1, 512, 784)
        square("V", 1, 784, 1024)
        quantise(1, 0)
        read(0)
        square("G", 2, 256, 344)
        square("G", 2, 344, 424)
        square("G", 2, 424, 512)
        square("G", 2, 768, 856)
        square("G", 2, 856, 936)
        square("G", 2, 936, 1024)
        quantise(1, 1)
        finish(0)
        read(1)
        square("S", 2, 0, 128)
        finish(1)
        read(2)
        square("S", 2, 128, 256)
        finish(2)
        read(3)
        square("S", 2, 512, 640)
        quantise(2, 0)
        finish(3)
        read(4)
        square("S", 2, 640, 768)
        finish(4)
        read(5)
        quantise(2, 1)
        finish(5)
        read(6)
        finish(6)
        read(7)
        finish(7)
        read(8)
        finish(8)
        read(9)
        finish(9)
        read(10)
        finish(10)
        read(11)
        finish(11)
